import numpy as np
import ml_dtypes


def mxq(x, axis, fmt="e4m3"):
    dtype, down = {"e4m3": (ml_dtypes.float8_e4m3fn, 7), "e5m2": (ml_dtypes.float8_e5m2, 14)}[fmt]
    v = np.moveaxis(np.asarray(x, np.float32).astype(ml_dtypes.bfloat16).astype(np.float64), axis, -1)
    blocks = v.reshape(v.shape[:-1] + (-1, 32))
    amax = np.abs(blocks).max(-1, keepdims=True)
    byte = np.maximum(np.where(amax > 0, np.frexp(amax)[1] - 1 + 127, 0) - down, 1)
    scale = np.exp2(byte - 127.0)
    codes = (blocks / scale).astype(np.float32).astype(dtype).astype(np.float64)
    return np.moveaxis((codes * scale).reshape(v.shape), -1, axis)


WIDE = False


def mx_kscale(k):
    if not WIDE:
        return np.ones(k)
    levels = np.array([10, -10, 5, -5, 0])
    if k % 512:
        return np.exp2(np.random.permutation(np.resize(levels, k // 32))).repeat(32)
    a = np.empty((k // 512, 16))
    for p in range(k // 512):
        a[p, :8] = np.random.permutation(np.resize(levels, 8))
        for g in range(8):
            far = levels[np.abs(levels - a[p, g]) >= 10]
            a[p, g + 8] = far[np.random.randint(len(far))]
    return np.exp2(a.ravel()).repeat(32)


BF16 = ml_dtypes.bfloat16


def bf(x):
    return np.asarray(x, np.float32).astype(BF16)


def f64(x):
    return np.asarray(x).astype(np.float64)


B, N1, N2, D, H, E = 32, 15, 17, 1024, 2, 64
N = N1 * N2 + 1
NDIMS = 2
KMAX = E // (2 * NDIMS)
BASE = 10000.0
PMAX = 3.0


def rope2d(xh, pos0, pos1):
    theta = 1.0 / (BASE ** (np.arange(KMAX) / KMAX))
    ang0 = np.broadcast_to(pos0[:, :, None, None] * theta, (B, N1, N2, KMAX))
    ang1 = np.broadcast_to(pos1[:, None, :, None] * theta, (B, N1, N2, KMAX))
    ang = np.concatenate([ang0, ang1], axis=-1).reshape(B, N - 1, 1, E // 2)
    cos, sin = np.cos(ang), np.sin(ang)
    t = xh[:, 1:]
    tr, ti = t[..., 0::2], t[..., 1::2]
    rr = tr * cos - ti * sin
    ri = tr * sin + ti * cos
    rot = np.stack([rr, ri], axis=-1).reshape(B, N - 1, H, E)
    return np.concatenate([xh[:, :1], rot], axis=1)


def setup_inputs():
    s = mx_kscale(D)
    return {"x": bf(np.random.standard_normal((B, N, D)) * s),
            "pos0": bf(np.random.uniform(-1.0, 1.0, (B, N1)) * PMAX),
            "pos1": bf(np.random.uniform(-1.0, 1.0, (B, N2)) * PMAX),
            "wq": bf(np.random.standard_normal((H * E, D)) * 1.5 / np.sqrt(D) / s),
            "wk": bf(np.random.standard_normal((H * E, D)) * 1.5 / np.sqrt(D) / s)}


def reference(x, pos0, pos1, wq, wk):
    xq = mxq(f64(x), 2, "e4m3")
    q = (xq @ mxq(f64(wq), 1, "e4m3").T).reshape(B, N, H, E)
    k = (xq @ mxq(f64(wk), 1, "e4m3").T).reshape(B, N, H, E)
    p0, p1 = f64(pos0), f64(pos1)
    return rope2d(q, p0, p1), rope2d(k, p0, p1)

@@ -1,0 +1,273 @@
+from contextlib import ExitStack
+
+import concourse.mybir as mybir
+from concourse.masks import make_identity
+
+F32 = mybir.dt.float32
+BF16 = mybir.dt.bfloat16
+U32 = mybir.dt.uint32
+U8 = mybir.dt.uint8
+FP8X4 = mybir.dt.float8_e4m3fn_x4
+ALU = mybir.AluOpType
+ACT = mybir.ActivationFunctionType
+
+P = 128
+BATCH, ROWS, COLS = 32, 15, 17
+TOKENS = 256
+DIM = 1024
+HEADS, PAIRS = 2, 32
+FEATURES = HEADS * PAIRS * 2
+FREQS = PAIRS // 2
+BASE = 10000.0
+
+QUARTERS = P // BATCH
+TILES = TOKENS // QUARTERS
+PACK = 4
+PASSES = DIM // (P * PACK)
+WORD_TILES = DIM // (2 * P)
+STEP_TILES = 4
+STEPS = TILES // STEP_TILES
+BANK_TILES = 2
+STEP_BANKS = STEP_TILES // BANK_TILES
+LOADS_AHEAD = 7
+TRIG_STEPS = 4
+TRIG_TILES = TRIG_STEPS * STEP_TILES
+TRIG_PARTS = TILES // TRIG_TILES
+
+FLOPS = 2 * BATCH * TOKENS * DIM * 2 * FEATURES
+
+
+def transpose_rows(nc, psum, rows, identity):
+    words = rows.bitcast(F32)
+    flipped = psum.tile([P, WORD_TILES, P], F32)
+    for g in range(PASSES):
+        for u in range(2):
+            nc.tensor.transpose(
+                flipped[:, 2 * g + u, :], words[:, 2 * P * g + u : 2 * P * (g + 1) : 2], identity
+            )
+    return flipped
+
+
+def group_pairs(copy, grouped, flipped):
+    copy(
+        out=grouped.bitcast(F32),
+        in_=flipped[:].rearrange("p (g u) r -> p g r u", u=2),
+    )
+
+
+def tile_attention_pa_t_kernel(tc, x, pos0, pos1, wq, wk, out_0, out_1):
+    nc = tc.nc
+    x_view = x.rearrange("b (r t) k -> (b r) t k", t=TILES)
+    out_views = [o.rearrange("b (r t) h f -> (b r) t (h f)", t=TILES) for o in (out_0, out_1)]
+
+    with ExitStack() as ctx:
+        ctx.enter_context(tc.manual_schedule())
+        const = ctx.enter_context(tc.tile_pool(name="const", bufs=1))
+        x_pool = ctx.enter_context(tc.tile_pool(name="x_rows", bufs=LOADS_AHEAD + 1))
+        work = ctx.enter_context(tc.tile_pool(name="work", bufs=3))
+        flip_psum = ctx.enter_context(tc.psum_pool(name="flip_psum", bufs=4))
+
+        pos0_rows = const.tile([BATCH, ROWS], BF16)
+        pos1_rows = const.tile([BATCH, COLS], BF16)
+        nc.sync.dma_start(out=pos0_rows[:], in_=pos0)
+        nc.sync.dma_start(out=pos1_rows[:], in_=pos1)
+        w_rows = const.tile([P, 2, DIM], BF16)
+        nc.sync.dma_start(out=w_rows[:, 0, :], in_=wq)
+        nc.sync.dma_start(out=w_rows[:, 1, :], in_=wk)
+
+        x_rows = {}
+
+        def load(step):
+            rows = x_pool.tile([P, STEP_TILES, DIM], BF16, name="rows")
+            nc.sync.dma_start(out=rows[:], in_=x_view[:, step * STEP_TILES : (step + 1) * STEP_TILES, :])
+            x_rows[step] = rows
+
+        for step in range(LOADS_AHEAD):
+            load(step)
+
+        ones = const.tile([P, 1], F32)
+        nc.vector.memset(ones[:], 1.0)
+        first_sin = const.tile([P, 1], F32)
+        nc.scalar.activation(out=first_sin[:], in_=ones[:], func=ACT.Sin)
+        identity = const.tile([P, P], F32)
+        make_identity(nc, identity[:])
+        send = const.tile([P, QUARTERS, BATCH, QUARTERS], BF16)
+        nc.vector.memset(send[:], 0.0)
+        for r in range(QUARTERS):
+            nc.vector.tensor_copy(out=send[:, r, :, r], in_=identity[:, 0:BATCH])
+
+        coords = const.tile([P, 2, TOKENS], BF16)
+        nc.vector.memset(coords[:], 0.0)
+        nc.vector.tensor_copy(
+            out=coords[0:BATCH, 0, 1:TOKENS].rearrange("b (i j) -> b i j", j=COLS),
+            in_=pos0_rows[:].unsqueeze(2).to_broadcast([BATCH, ROWS, COLS]),
+        )
+        nc.vector.tensor_copy(
+            out=coords[0:BATCH, 1, 1:TOKENS].rearrange("b (i j) -> b i j", j=COLS),
+            in_=pos1_rows[:].unsqueeze(1).to_broadcast([BATCH, ROWS, COLS]),
+        )
+        theta = const.tile([P, FREQS], F32)
+        for m in range(FREQS):
+            nc.vector.tensor_scalar(
+                out=theta[:, m : m + 1], in0=ones[:], scalar1=1.0 / BASE ** (m / FREQS), scalar2=None, op0=ALU.mult
+            )
+        own_coords = const.tile([P, 2, TILES], F32)
+        with tc.psum_pool(name="coord_psum", bufs=1) as coord_psum:
+            sent = coord_psum.tile([P, 2, TILES], F32)
+            for axis in range(2):
+                for r in range(QUARTERS):
+                    nc.tensor.matmul(
+                        out=sent[:, axis, :],
+                        lhsT=send[:, r, :, :].rearrange("k b q -> k (b q)"),
+                        rhs=coords[:, axis, r * TILES : (r + 1) * TILES],
+                        start=(r == 0),
+                        stop=(r == QUARTERS - 1),
+                    )
+            nc.vector.tensor_copy(out=own_coords[:], in_=sent[:])
+        prod_psum = ctx.enter_context(tc.psum_pool(name="prod_psum", bufs=2 * STEP_BANKS))
+
+        angle = const.tile([P, TILES, 2, FREQS], F32)
+        trig = const.tile([P, TILES, 3, PAIRS], F32)
+        half_sin_squares = {}
+
+        def part_tiles(part):
+            return slice(part * TRIG_TILES, (part + 1) * TRIG_TILES)
+
+        def angles(part):
+            spread = [P, TRIG_TILES, 2, FREQS]
+            nc.vector.tensor_tensor(
+                out=angle[:, part_tiles(part)],
+                in0=own_coords[:, :, part_tiles(part)].rearrange("p a t -> p t a").unsqueeze(3).to_broadcast(spread),
+                in1=theta[:].unsqueeze(1).unsqueeze(2).to_broadcast(spread),
+                op=ALU.mult,
+            )
+
+        def sines(part):
+            tiles = part_tiles(part)
+            angle_pairs = angle[:, tiles].rearrange("p t a m -> p t (a m)")
+            half_sin = work.tile([P, TRIG_TILES, PAIRS], F32, name="half_sin")
+            half_sin_sq = work.tile([P, TRIG_TILES, PAIRS], F32, name="half_sin_sq")
+            nc.scalar.activation(out=half_sin[:], in_=angle_pairs, func=ACT.Sin, scale=0.5)
+            nc.scalar.activation(out=half_sin_sq[:], in_=half_sin[:], func=ACT.Square)
+            nc.scalar.activation(out=trig[:, tiles, 2, :], in_=angle_pairs, func=ACT.Sin)
+            nc.scalar.activation(out=trig[:, tiles, 0, :], in_=angle_pairs, func=ACT.Sin, scale=-1.0)
+            half_sin_squares[part] = half_sin_sq
+
+        def cosines(part):
+            nc.vector.tensor_scalar(
+                out=trig[:, part_tiles(part), 1, :],
+                in0=half_sin_squares[part][:],
+                scalar1=-2.0,
+                scalar2=1.0,
+                op0=ALU.mult,
+                op1=ALU.add,
+            )
+
+        angles(0)
+        sines(0)
+
+        w_grouped = const.tile([P, PASSES, 2, P, PACK], BF16, align_bytes=64)
+        for which in range(2):
+            flipped = transpose_rows(nc, flip_psum, w_rows[:, which, :], identity[:])
+            group_pairs(nc.vector.tensor_copy, w_grouped[:, :, which, :, :], flipped)
+        w_codes = const.tile([P, PASSES, 2 * P], U32, align_bytes=64)
+        w_scales = const.tile([P, PASSES, 2 * P], U8, align_bytes=64)
+        nc.vector.quantize_mx(
+            out=w_codes[:].rearrange("p g n -> p (g n)").bitcast(FP8X4),
+            scales=w_scales[:].rearrange("p g n -> p (g n)"),
+            in_=w_grouped[:].rearrange("p g w n j -> p (g w n j)"),
+        )
+        for part in range(1, TRIG_PARTS):
+            angles(part)
+        cosines(0)
+
+        grouped_rows = {}
+        quantised = {}
+        products = {}
+
+        def transpose_and_group(step):
+            grouped = work.tile([P, STEP_TILES, PASSES, P, PACK], BF16, align_bytes=64, name="grouped")
+            for i in range(STEP_TILES):
+                flipped = transpose_rows(nc, flip_psum, x_rows[step][:, i, :], identity[:])
+                group_pairs(nc.scalar.copy, grouped[:, i], flipped)
+            grouped_rows[step] = grouped
+
+        def quantise(step):
+            codes = work.tile([P, STEP_TILES, PASSES, P], U32, align_bytes=64, name="codes")
+            scales = work.tile([P, STEP_TILES, PASSES, P], U8, align_bytes=64, name="scales")
+            nc.vector.quantize_mx(
+                out=codes[:].rearrange("p t g r -> p (t g r)").bitcast(FP8X4),
+                scales=scales[:].rearrange("p t g r -> p (t g r)"),
+                in_=grouped_rows[step][:].rearrange("p t g r j -> p (t g r j)"),
+            )
+            quantised[step] = (codes, scales)
+
+        def project(step):
+            codes, scales = quantised[step]
+            products[step] = []
+            for bank in range(STEP_BANKS):
+                product = prod_psum.tile([P, BANK_TILES, 2 * HEADS, PAIRS, 2], F32, name="product")
+                for j in range(BANK_TILES):
+                    i = bank * BANK_TILES + j
+                    for g in range(PASSES):
+                        nc.tensor.matmul_mx(
+                            out=product[:, j].rearrange("p c r e -> p (c r e)"),
+                            lhsT=codes[:, i, g, :].bitcast(FP8X4),
+                            lhsT_scale=scales[:, i, g, :],
+                            rhs=w_codes[:, g, :].bitcast(FP8X4),
+                            rhs_scale=w_scales[:, g, :],
+                            start=(g == 0),
+                            stop=(g == PASSES - 1),
+                        )
+                products[step].append(product)
+
+        def rotate_and_store(step, pieces):
+            spread = [P, 2 * HEADS, PAIRS, 2]
+            from_re = work.tile([P, STEP_TILES] + spread[1:], F32, name="from_re")
+            from_im = work.tile([P, STEP_TILES] + spread[1:], F32, name="from_im")
+            rotated = work.tile([P, 2, STEP_TILES, FEATURES], F32, name="rotated")
+            run = STEP_TILES // pieces
+            for first in range(0, STEP_TILES, run):
+                for i in range(first, first + run):
+                    product = products[step][i // BANK_TILES][:, i % BANK_TILES]
+                    t = step * STEP_TILES + i
+                    for part, result, low_row in ((0, from_re, 1), (1, from_im, 0)):
+                        nc.vector.tensor_tensor(
+                            out=result[:, i],
+                            in0=product[:, :, :, part : part + 1].to_broadcast(spread),
+                            in1=trig[:, t, low_row : low_row + 2, :]
+                            .rearrange("p e r -> p r e")
+                            .unsqueeze(1)
+                            .to_broadcast(spread),
+                            op=ALU.mult,
+                        )
+                tiles = slice(first, first + run)
+                nc.gpsimd.tensor_tensor(
+                    out=rotated[:, :, tiles].rearrange("p w t f -> p t w f"),
+                    in0=from_re[:, tiles].rearrange("p t (w h) r e -> p t w (h r e)", w=2),
+                    in1=from_im[:, tiles].rearrange("p t (w h) r e -> p t w (h r e)", w=2),
+                    op=ALU.add,
+                )
+                for which in range(2):
+                    nc.sync.dma_start(
+                        out=out_views[which][:, step * STEP_TILES + first : step * STEP_TILES + first + run, :],
+                        in_=rotated[:, which, tiles],
+                    )
+
+        for step in range(STEPS + 2):
+            next_part = step // TRIG_STEPS + 1
+            build_next_part = step % TRIG_STEPS == TRIG_STEPS - 1 and next_part < TRIG_PARTS
+            if step + LOADS_AHEAD < STEPS:
+                load(step + LOADS_AHEAD)
+            if step < STEPS:
+                transpose_and_group(step)
+            if build_next_part:
+                sines(next_part)
+            if 1 <= step <= STEPS:
+                project(step - 1)
+            if step >= 2:
+                rotate_and_store(step - 2, pieces=STEP_BANKS if step - 2 == STEPS - 1 else 1)
+            if step < STEPS:
+                quantise(step)
+            if build_next_part:
+                cosines(next_part)

@@ -26,13 +26,14 @@ PACK = 4
 PASSES = DIM // (P * PACK)
 WORD_TILES = DIM // (2 * P)
 STEP_TILES = 4
-STEPS = TILES // STEP_TILES
+SHORT_TILES = STEP_TILES // 2
+STEP_SIZES = [SHORT_TILES] * 2 + [STEP_TILES] * (TILES // STEP_TILES - 2) + [SHORT_TILES] * 2
+STEPS = len(STEP_SIZES)
+STEP_STARTS = [sum(STEP_SIZES[:step]) for step in range(STEPS)]
 BANK_TILES = 2
 STEP_BANKS = STEP_TILES // BANK_TILES
 LOADS_AHEAD = 7
-TRIG_STEPS = 4
-TRIG_TILES = TRIG_STEPS * STEP_TILES
-TRIG_PARTS = TILES // TRIG_TILES
+FIRST_ANGLES = 4 * STEP_TILES
 
 FLOPS = 2 * BATCH * TOKENS * DIM * 2 * FEATURES
 
@@ -75,11 +76,14 @@ def tile_attention_pa_t_kernel(tc, x, pos0, pos1, wq, wk, out_0, out_1):
         nc.sync.dma_start(out=w_rows[:, 0, :], in_=wq)
         nc.sync.dma_start(out=w_rows[:, 1, :], in_=wk)
 
+        def step_tiles(step):
+            return slice(STEP_STARTS[step], STEP_STARTS[step] + STEP_SIZES[step])
+
         x_rows = {}
 
         def load(step):
-            rows = x_pool.tile([P, STEP_TILES, DIM], BF16, name="rows")
-            nc.sync.dma_start(out=rows[:], in_=x_view[:, step * STEP_TILES : (step + 1) * STEP_TILES, :])
+            rows = x_pool.tile([P, STEP_SIZES[step], DIM], BF16, name="rows")
+            nc.sync.dma_start(out=rows[:], in_=x_view[:, step_tiles(step), :])
             x_rows[step] = rows
 
         for step in range(LOADS_AHEAD):
@@ -130,41 +134,37 @@ def tile_attention_pa_t_kernel(tc, x, pos0, pos1, wq, wk, out_0, out_1):
         trig = const.tile([P, TILES, 3, PAIRS], F32)
         half_sin_squares = {}
 
-        def part_tiles(part):
-            return slice(part * TRIG_TILES, (part + 1) * TRIG_TILES)
-
-        def angles(part):
-            spread = [P, TRIG_TILES, 2, FREQS]
+        def angles(tiles):
+            spread = [P, tiles.stop - tiles.start, 2, FREQS]
             nc.vector.tensor_tensor(
-                out=angle[:, part_tiles(part)],
-                in0=own_coords[:, :, part_tiles(part)].rearrange("p a t -> p t a").unsqueeze(3).to_broadcast(spread),
+                out=angle[:, tiles],
+                in0=own_coords[:, :, tiles].rearrange("p a t -> p t a").unsqueeze(3).to_broadcast(spread),
                 in1=theta[:].unsqueeze(1).unsqueeze(2).to_broadcast(spread),
                 op=ALU.mult,
             )
 
-        def sines(part):
-            tiles = part_tiles(part)
+        def sines(step):
+            tiles = step_tiles(step)
             angle_pairs = angle[:, tiles].rearrange("p t a m -> p t (a m)")
-            half_sin = work.tile([P, TRIG_TILES, PAIRS], F32, name="half_sin")
-            half_sin_sq = work.tile([P, TRIG_TILES, PAIRS], F32, name="half_sin_sq")
+            half_sin = work.tile([P, STEP_SIZES[step], PAIRS], F32, name="half_sin")
+            half_sin_sq = work.tile([P, STEP_SIZES[step], PAIRS], F32, name="half_sin_sq")
             nc.scalar.activation(out=half_sin[:], in_=angle_pairs, func=ACT.Sin, scale=0.5)
             nc.scalar.activation(out=half_sin_sq[:], in_=half_sin[:], func=ACT.Square)
             nc.scalar.activation(out=trig[:, tiles, 2, :], in_=angle_pairs, func=ACT.Sin)
             nc.scalar.activation(out=trig[:, tiles, 0, :], in_=angle_pairs, func=ACT.Sin, scale=-1.0)
-            half_sin_squares[part] = half_sin_sq
+            half_sin_squares[step] = half_sin_sq
 
-        def cosines(part):
-            nc.vector.tensor_scalar(
-                out=trig[:, part_tiles(part), 1, :],
-                in0=half_sin_squares[part][:],
+        def cosines(step):
+            nc.gpsimd.tensor_scalar(
+                out=trig[:, step_tiles(step), 1, :],
+                in0=half_sin_squares[step][:],
                 scalar1=-2.0,
                 scalar2=1.0,
                 op0=ALU.mult,
                 op1=ALU.add,
             )
 
-        angles(0)
-        sines(0)
+        angles(slice(0, FIRST_ANGLES))
 
         w_grouped = const.tile([P, PASSES, 2, P, PACK], BF16, align_bytes=64)
         for which in range(2):
@@ -177,24 +177,21 @@ def tile_attention_pa_t_kernel(tc, x, pos0, pos1, wq, wk, out_0, out_1):
             scales=w_scales[:].rearrange("p g n -> p (g n)"),
             in_=w_grouped[:].rearrange("p g w n j -> p (g w n j)"),
         )
-        for part in range(1, TRIG_PARTS):
-            angles(part)
-        cosines(0)
 
         grouped_rows = {}
         quantised = {}
         products = {}
 
         def transpose_and_group(step):
-            grouped = work.tile([P, STEP_TILES, PASSES, P, PACK], BF16, align_bytes=64, name="grouped")
-            for i in range(STEP_TILES):
+            grouped = work.tile([P, STEP_SIZES[step], PASSES, P, PACK], BF16, align_bytes=64, name="grouped")
+            for i in range(STEP_SIZES[step]):
                 flipped = transpose_rows(nc, flip_psum, x_rows[step][:, i, :], identity[:])
                 group_pairs(nc.scalar.copy, grouped[:, i], flipped)
             grouped_rows[step] = grouped
 
         def quantise(step):
-            codes = work.tile([P, STEP_TILES, PASSES, P], U32, align_bytes=64, name="codes")
-            scales = work.tile([P, STEP_TILES, PASSES, P], U8, align_bytes=64, name="scales")
+            codes = work.tile([P, STEP_SIZES[step], PASSES, P], U32, align_bytes=64, name="codes")
+            scales = work.tile([P, STEP_SIZES[step], PASSES, P], U8, align_bytes=64, name="scales")
             nc.vector.quantize_mx(
                 out=codes[:].rearrange("p t g r -> p (t g r)").bitcast(FP8X4),
                 scales=scales[:].rearrange("p t g r -> p (t g r)"),
@@ -205,7 +202,7 @@ def tile_attention_pa_t_kernel(tc, x, pos0, pos1, wq, wk, out_0, out_1):
         def project(step):
             codes, scales = quantised[step]
             products[step] = []
-            for bank in range(STEP_BANKS):
+            for bank in range(STEP_SIZES[step] // BANK_TILES):
                 product = prod_psum.tile([P, BANK_TILES, 2 * HEADS, PAIRS, 2], F32, name="product")
                 for j in range(BANK_TILES):
                     i = bank * BANK_TILES + j
@@ -223,14 +220,15 @@ def tile_attention_pa_t_kernel(tc, x, pos0, pos1, wq, wk, out_0, out_1):
 
         def rotate_and_store(step, pieces):
             spread = [P, 2 * HEADS, PAIRS, 2]
-            from_re = work.tile([P, STEP_TILES] + spread[1:], F32, name="from_re")
-            from_im = work.tile([P, STEP_TILES] + spread[1:], F32, name="from_im")
-            rotated = work.tile([P, 2, STEP_TILES, FEATURES], F32, name="rotated")
-            run = STEP_TILES // pieces
-            for first in range(0, STEP_TILES, run):
+            size = STEP_SIZES[step]
+            from_re = work.tile([P, size] + spread[1:], F32, name="from_re")
+            from_im = work.tile([P, size] + spread[1:], F32, name="from_im")
+            rotated = work.tile([P, 2, size, FEATURES], F32, name="rotated")
+            run = size // pieces
+            for first in range(0, size, run):
                 for i in range(first, first + run):
                     product = products[step][i // BANK_TILES][:, i % BANK_TILES]
-                    t = step * STEP_TILES + i
+                    t = STEP_STARTS[step] + i
                     for part, result, low_row in ((0, from_re, 1), (1, from_im, 0)):
                         nc.vector.tensor_tensor(
                             out=result[:, i],
@@ -242,7 +240,8 @@ def tile_attention_pa_t_kernel(tc, x, pos0, pos1, wq, wk, out_0, out_1):
                             op=ALU.mult,
                         )
                 tiles = slice(first, first + run)
-                nc.gpsimd.tensor_tensor(
+                adder = nc.vector if step == STEPS - 1 and first + run == size else nc.gpsimd
+                adder.tensor_tensor(
                     out=rotated[:, :, tiles].rearrange("p w t f -> p t w f"),
                     in0=from_re[:, tiles].rearrange("p t (w h) r e -> p t w (h r e)", w=2),
                     in1=from_im[:, tiles].rearrange("p t (w h) r e -> p t w (h r e)", w=2),
@@ -250,24 +249,24 @@ def tile_attention_pa_t_kernel(tc, x, pos0, pos1, wq, wk, out_0, out_1):
                 )
                 for which in range(2):
                     nc.sync.dma_start(
-                        out=out_views[which][:, step * STEP_TILES + first : step * STEP_TILES + first + run, :],
+                        out=out_views[which][:, STEP_STARTS[step] + first : STEP_STARTS[step] + first + run, :],
                         in_=rotated[:, which, tiles],
                     )
 
         for step in range(STEPS + 2):
-            next_part = step // TRIG_STEPS + 1
-            build_next_part = step % TRIG_STEPS == TRIG_STEPS - 1 and next_part < TRIG_PARTS
             if step + LOADS_AHEAD < STEPS:
                 load(step + LOADS_AHEAD)
             if step < STEPS:
                 transpose_and_group(step)
-            if build_next_part:
-                sines(next_part)
+                for ahead in range(step + 1 if step else 0, min(step + 2, STEPS)):
+                    sines(ahead)
             if 1 <= step <= STEPS:
                 project(step - 1)
             if step >= 2:
-                rotate_and_store(step - 2, pieces=STEP_BANKS if step - 2 == STEPS - 1 else 1)
+                rotate_and_store(step - 2, pieces=SHORT_TILES if step - 2 == STEPS - 1 else 1)
             if step < STEPS:
                 quantise(step)
-            if build_next_part:
-                cosines(next_part)
+                for ahead in range(step + 1 if step else 0, min(step + 2, STEPS)):
+                    cosines(ahead)
+            if step == 0:
+                angles(slice(FIRST_ANGLES, TILES))

@@ -1,3 +1,4 @@
+import math
 from contextlib import ExitStack
 
 import concourse.mybir as mybir
@@ -91,6 +92,8 @@ def tile_attention_pa_t_kernel(tc, x, pos0, pos1, wq, wk, out_0, out_1):
 
         ones = const.tile([P, 1], F32)
         nc.vector.memset(ones[:], 1.0)
+        quarter_turn = const.tile([P, 1], F32)
+        nc.vector.tensor_scalar(out=quarter_turn[:], in0=ones[:], scalar1=math.pi / 2, scalar2=None, op0=ALU.mult)
         first_sin = const.tile([P, 1], F32)
         nc.scalar.activation(out=first_sin[:], in_=ones[:], func=ACT.Sin)
         identity = const.tile([P, P], F32)
@@ -132,8 +135,6 @@ def tile_attention_pa_t_kernel(tc, x, pos0, pos1, wq, wk, out_0, out_1):
 
         angle = const.tile([P, TILES, 2, FREQS], F32)
         trig = const.tile([P, TILES, 3, PAIRS], F32)
-        half_sin_squares = {}
-
         def angles(tiles):
             spread = [P, tiles.stop - tiles.start, 2, FREQS]
             nc.vector.tensor_tensor(
@@ -146,22 +147,12 @@ def tile_attention_pa_t_kernel(tc, x, pos0, pos1, wq, wk, out_0, out_1):
         def sines(step):
             tiles = step_tiles(step)
             angle_pairs = angle[:, tiles].rearrange("p t a m -> p t (a m)")
-            half_sin = work.tile([P, STEP_SIZES[step], PAIRS], F32, name="half_sin")
-            half_sin_sq = work.tile([P, STEP_SIZES[step], PAIRS], F32, name="half_sin_sq")
-            nc.scalar.activation(out=half_sin[:], in_=angle_pairs, func=ACT.Sin, scale=0.5)
-            nc.scalar.activation(out=half_sin_sq[:], in_=half_sin[:], func=ACT.Square)
+            magnitude = work.tile([P, STEP_SIZES[step], PAIRS], F32, name="magnitude")
+            nc.scalar.activation(out=magnitude[:], in_=angle_pairs, func=ACT.Abs)
             nc.scalar.activation(out=trig[:, tiles, 2, :], in_=angle_pairs, func=ACT.Sin)
             nc.scalar.activation(out=trig[:, tiles, 0, :], in_=angle_pairs, func=ACT.Sin, scale=-1.0)
-            half_sin_squares[step] = half_sin_sq
-
-        def cosines(step):
-            nc.gpsimd.tensor_scalar(
-                out=trig[:, step_tiles(step), 1, :],
-                in0=half_sin_squares[step][:],
-                scalar1=-2.0,
-                scalar2=1.0,
-                op0=ALU.mult,
-                op1=ALU.add,
+            nc.scalar.activation(
+                out=trig[:, tiles, 1, :], in_=magnitude[:], func=ACT.Sin, scale=-1.0, bias=quarter_turn[:]
             )
 
         angles(slice(0, FIRST_ANGLES))
@@ -266,7 +257,5 @@ def tile_attention_pa_t_kernel(tc, x, pos0, pos1, wq, wk, out_0, out_1):
                 rotate_and_store(step - 2, pieces=SHORT_TILES if step - 2 == STEPS - 1 else 1)
             if step < STEPS:
                 quantise(step)
-                for ahead in range(step + 1 if step else 0, min(step + 2, STEPS)):
-                    cosines(ahead)
             if step == 0:
                 angles(slice(FIRST_ANGLES, TILES))

@@ -67,6 +67,7 @@ def tile_attention_pa_t_kernel(tc, x, pos0, pos1, wq, wk, out_0, out_1):
         const = ctx.enter_context(tc.tile_pool(name="const", bufs=1))
         x_pool = ctx.enter_context(tc.tile_pool(name="x_rows", bufs=LOADS_AHEAD + 1))
         work = ctx.enter_context(tc.tile_pool(name="work", bufs=3))
+        out_pool = ctx.enter_context(tc.tile_pool(name="out_rows", bufs=5))
         flip_psum = ctx.enter_context(tc.psum_pool(name="flip_psum", bufs=4))
 
         pos0_rows = const.tile([BATCH, ROWS], BF16)
@@ -209,40 +210,50 @@ def tile_attention_pa_t_kernel(tc, x, pos0, pos1, wq, wk, out_0, out_1):
                         )
                 products[step].append(product)
 
-        def rotate_and_store(step, pieces):
+        def multiply(step, i, results):
+            product = products[step][i // BANK_TILES][:, i % BANK_TILES]
             spread = [P, 2 * HEADS, PAIRS, 2]
-            size = STEP_SIZES[step]
-            from_re = work.tile([P, size] + spread[1:], F32, name="from_re")
-            from_im = work.tile([P, size] + spread[1:], F32, name="from_im")
-            rotated = work.tile([P, 2, size, FEATURES], F32, name="rotated")
-            run = size // pieces
-            for first in range(0, size, run):
-                for i in range(first, first + run):
-                    product = products[step][i // BANK_TILES][:, i % BANK_TILES]
-                    t = STEP_STARTS[step] + i
-                    for part, result, low_row in ((0, from_re, 1), (1, from_im, 0)):
-                        nc.vector.tensor_tensor(
-                            out=result[:, i],
-                            in0=product[:, :, :, part : part + 1].to_broadcast(spread),
-                            in1=trig[:, t, low_row : low_row + 2, :]
-                            .rearrange("p e r -> p r e")
-                            .unsqueeze(1)
-                            .to_broadcast(spread),
-                            op=ALU.mult,
-                        )
-                tiles = slice(first, first + run)
-                adder = nc.vector if step == STEPS - 1 and first + run == size else nc.gpsimd
-                adder.tensor_tensor(
-                    out=rotated[:, :, tiles].rearrange("p w t f -> p t w f"),
-                    in0=from_re[:, tiles].rearrange("p t (w h) r e -> p t w (h r e)", w=2),
-                    in1=from_im[:, tiles].rearrange("p t (w h) r e -> p t w (h r e)", w=2),
-                    op=ALU.add,
+            for part, result, low_row in ((0, results[0], 1), (1, results[1], 0)):
+                nc.vector.tensor_tensor(
+                    out=result[:, i],
+                    in0=product[:, :, :, part : part + 1].to_broadcast(spread),
+                    in1=trig[:, STEP_STARTS[step] + i, low_row : low_row + 2, :]
+                    .rearrange("p e r -> p r e")
+                    .unsqueeze(1)
+                    .to_broadcast(spread),
+                    op=ALU.mult,
                 )
-                for which in range(2):
-                    nc.sync.dma_start(
-                        out=out_views[which][:, STEP_STARTS[step] + first : STEP_STARTS[step] + first + run, :],
-                        in_=rotated[:, which, tiles],
-                    )
+
+        def add_and_store(engine, step, results, rotated):
+            engine.tensor_tensor(
+                out=rotated[:].rearrange("p w t f -> p t w f"),
+                in0=results[0][:].rearrange("p t (w h) r e -> p t w (h r e)", w=2),
+                in1=results[1][:].rearrange("p t (w h) r e -> p t w (h r e)", w=2),
+                op=ALU.add,
+            )
+            for which in range(2):
+                nc.sync.dma_start(out=out_views[which][:, step_tiles(step), :], in_=rotated[:, which])
+
+        pending = []
+
+        def rotate_and_store(step):
+            size = STEP_SIZES[step]
+            results = [
+                work.tile([P, size, 2 * HEADS, PAIRS, 2], F32, name="from_re"),
+                work.tile([P, size, 2 * HEADS, PAIRS, 2], F32, name="from_im"),
+            ]
+            rotated = out_pool.tile([P, 2, size, FEATURES], F32, name="rotated")
+            for i in range(size):
+                multiply(step, i, results)
+            if size == STEP_TILES:
+                add_and_store(nc.gpsimd, step, results, rotated)
+            elif step < STEPS // 2:
+                add_and_store(nc.vector, step, results, rotated)
+            else:
+                pending.append((step, results, rotated))
+            if step == STEPS - 1:
+                for late in pending:
+                    add_and_store(nc.vector, *late)
 
         for step in range(STEPS + 2):
             if step + LOADS_AHEAD < STEPS:
@@ -254,7 +265,7 @@ def tile_attention_pa_t_kernel(tc, x, pos0, pos1, wq, wk, out_0, out_1):
             if 1 <= step <= STEPS:
                 project(step - 1)
             if step >= 2:
-                rotate_and_store(step - 2, pieces=SHORT_TILES if step - 2 == STEPS - 1 else 1)
+                rotate_and_store(step - 2)
             if step < STEPS:
                 quantise(step)
             if step == 0:

@@ -33,6 +33,7 @@ STEPS = len(STEP_SIZES)
 STEP_STARTS = [sum(STEP_SIZES[:step]) for step in range(STEPS)]
 BANK_TILES = 2
 STEP_BANKS = STEP_TILES // BANK_TILES
+WARM_COLUMNS = 512
 LOADS_AHEAD = 7
 FIRST_ANGLES = 4 * STEP_TILES
 
@@ -91,6 +92,8 @@ def tile_attention_pa_t_kernel(tc, x, pos0, pos1, wq, wk, out_0, out_1):
         for step in range(LOADS_AHEAD):
             load(step)
 
+        zeros = const.tile([P, WARM_COLUMNS], BF16)
+        nc.vector.memset(zeros[:], 0.0)
         ones = const.tile([P, 1], F32)
         nc.vector.memset(ones[:], 1.0)
         quarter_turn = const.tile([P, 1], F32)
@@ -121,6 +124,15 @@ def tile_attention_pa_t_kernel(tc, x, pos0, pos1, wq, wk, out_0, out_1):
             )
         own_coords = const.tile([P, 2, TILES], F32)
         with tc.psum_pool(name="coord_psum", bufs=1) as coord_psum:
+            idle_product = coord_psum.tile([P, WARM_COLUMNS], F32)
+
+            def keep_clock_up(count):
+                for turn in range(count):
+                    nc.tensor.matmul(
+                        out=idle_product[:], lhsT=zeros[:, 0:P], rhs=zeros[:], start=True, stop=True
+                    )
+
+            keep_clock_up(5)
             sent = coord_psum.tile([P, 2, TILES], F32)
             for axis in range(2):
                 for r in range(QUARTERS):
@@ -131,6 +143,7 @@ def tile_attention_pa_t_kernel(tc, x, pos0, pos1, wq, wk, out_0, out_1):
                         start=(r == 0),
                         stop=(r == QUARTERS - 1),
                     )
+            keep_clock_up(3)
             nc.vector.tensor_copy(out=own_coords[:], in_=sent[:])
         prod_psum = ctx.enter_context(tc.psum_pool(name="prod_psum", bufs=2 * STEP_BANKS))
 

@@ -28,7 +28,7 @@ PASSES = DIM // (P * PACK)
 WORD_TILES = DIM // (2 * P)
 STEP_TILES = 4
 SHORT_TILES = STEP_TILES // 2
-STEP_SIZES = [SHORT_TILES] * 2 + [STEP_TILES] * (TILES // STEP_TILES - 2) + [SHORT_TILES] * 2
+STEP_SIZES = [STEP_TILES] * (TILES // STEP_TILES - 1) + [SHORT_TILES] * 2
 STEPS = len(STEP_SIZES)
 STEP_STARTS = [sum(STEP_SIZES[:step]) for step in range(STEPS)]
 BANK_TILES = 2
@@ -86,7 +86,10 @@ def tile_attention_pa_t_kernel(tc, x, pos0, pos1, wq, wk, out_0, out_1):
 
         def load(step):
             rows = x_pool.tile([P, STEP_SIZES[step], DIM], BF16, name="rows")
-            nc.sync.dma_start(out=rows[:], in_=x_view[:, step_tiles(step), :])
+            run = 1 if step < 2 else STEP_SIZES[step]
+            for first in range(0, STEP_SIZES[step], run):
+                start = STEP_STARTS[step] + first
+                nc.sync.dma_start(out=rows[:, first : first + run, :], in_=x_view[:, start : start + run, :])
             x_rows[step] = rows
 
         for step in range(LOADS_AHEAD):
@@ -132,7 +135,7 @@ def tile_attention_pa_t_kernel(tc, x, pos0, pos1, wq, wk, out_0, out_1):
                         out=idle_product[:], lhsT=zeros[:, 0:P], rhs=zeros[:], start=True, stop=True
                     )
 
-            keep_clock_up(5)
+            keep_clock_up(4)
             sent = coord_psum.tile([P, 2, TILES], F32)
             for axis in range(2):
                 for r in range(QUARTERS):
@@ -197,11 +200,14 @@ def tile_attention_pa_t_kernel(tc, x, pos0, pos1, wq, wk, out_0, out_1):
         def quantise(step):
             codes = work.tile([P, STEP_SIZES[step], PASSES, P], U32, align_bytes=64, name="codes")
             scales = work.tile([P, STEP_SIZES[step], PASSES, P], U8, align_bytes=64, name="scales")
-            nc.vector.quantize_mx(
-                out=codes[:].rearrange("p t g r -> p (t g r)").bitcast(FP8X4),
-                scales=scales[:].rearrange("p t g r -> p (t g r)"),
-                in_=grouped_rows[step][:].rearrange("p t g r j -> p (t g r j)"),
-            )
+            run = SHORT_TILES if step == 0 else STEP_SIZES[step]
+            for first in range(0, STEP_SIZES[step], run):
+                tiles = slice(first, first + run)
+                nc.vector.quantize_mx(
+                    out=codes[:, tiles].rearrange("p t g r -> p (t g r)").bitcast(FP8X4),
+                    scales=scales[:, tiles].rearrange("p t g r -> p (t g r)"),
+                    in_=grouped_rows[step][:, tiles].rearrange("p t g r j -> p (t g r j)"),
+                )
             quantised[step] = (codes, scales)
 
         def project(step):
@@ -260,8 +266,6 @@ def tile_attention_pa_t_kernel(tc, x, pos0, pos1, wq, wk, out_0, out_1):
                 multiply(step, i, results)
             if size == STEP_TILES:
                 add_and_store(nc.gpsimd, step, results, rotated)
-            elif step < STEPS // 2:
-                add_and_store(nc.vector, step, results, rotated)
             else:
                 pending.append((step, results, rotated))
             if step == STEPS - 1:
@@ -273,9 +277,8 @@ def tile_attention_pa_t_kernel(tc, x, pos0, pos1, wq, wk, out_0, out_1):
                 load(step + LOADS_AHEAD)
             if step < STEPS:
                 transpose_and_group(step)
-                for ahead in range(step + 1 if step else 0, min(step + 2, STEPS)):
-                    sines(ahead)
             if 1 <= step <= STEPS:
+                sines(step - 1)
                 project(step - 1)
             if step >= 2:
                 rotate_and_store(step - 2)

@@ -34,20 +34,22 @@ STEP_STARTS = [sum(STEP_SIZES[:step]) for step in range(STEPS)]
 BANK_TILES = 2
 STEP_BANKS = STEP_TILES // BANK_TILES
 WARM_COLUMNS = 512
+LATE_ANGLES = 12 * STEP_TILES
 LOADS_AHEAD = 7
 FIRST_ANGLES = 4 * STEP_TILES
 
 FLOPS = 2 * BATCH * TOKENS * DIM * 2 * FEATURES
 
 
-def transpose_rows(nc, psum, rows, identity):
-    words = rows.bitcast(F32)
+def split_words(rows):
+    return rows.bitcast(F32).rearrange("p (g w u) -> p g u w", g=PASSES, u=2)
+
+
+def transpose_rows(nc, psum, words, identity):
     flipped = psum.tile([P, WORD_TILES, P], F32)
     for g in range(PASSES):
         for u in range(2):
-            nc.tensor.transpose(
-                flipped[:, 2 * g + u, :], words[:, 2 * P * g + u : 2 * P * (g + 1) : 2], identity
-            )
+            nc.tensor.transpose(flipped[:, 2 * g + u, :], words[:, g, u, :], identity)
     return flipped
 
 
@@ -176,7 +178,7 @@ def tile_attention_pa_t_kernel(tc, x, pos0, pos1, wq, wk, out_0, out_1):
 
         w_grouped = const.tile([P, PASSES, 2, P, PACK], BF16, align_bytes=64)
         for which in range(2):
-            flipped = transpose_rows(nc, flip_psum, w_rows[:, which, :], identity[:])
+            flipped = transpose_rows(nc, flip_psum, split_words(w_rows[:, which, :]), identity[:])
             group_pairs(nc.vector.tensor_copy, w_grouped[:, :, which, :, :], flipped)
         w_codes = const.tile([P, PASSES, 2 * P], U32, align_bytes=64)
         w_scales = const.tile([P, PASSES, 2 * P], U8, align_bytes=64)
@@ -190,10 +192,21 @@ def tile_attention_pa_t_kernel(tc, x, pos0, pos1, wq, wk, out_0, out_1):
         quantised = {}
         products = {}
 
+        sorted_words = {}
+
+        def sort_words(step):
+            words = work.tile([P, PASSES, 2, P], F32, name="words")
+            nc.scalar.copy(out=words[:], in_=split_words(x_rows[step][:, STEP_SIZES[step] - 1, :]))
+            sorted_words[step] = words
+
         def transpose_and_group(step):
             grouped = work.tile([P, STEP_SIZES[step], PASSES, P, PACK], BF16, align_bytes=64, name="grouped")
             for i in range(STEP_SIZES[step]):
-                flipped = transpose_rows(nc, flip_psum, x_rows[step][:, i, :], identity[:])
+                if step in sorted_words and i == STEP_SIZES[step] - 1:
+                    words = sorted_words[step][:]
+                else:
+                    words = split_words(x_rows[step][:, i, :])
+                flipped = transpose_rows(nc, flip_psum, words, identity[:])
                 group_pairs(nc.scalar.copy, grouped[:, i], flipped)
             grouped_rows[step] = grouped
 
@@ -279,10 +292,15 @@ def tile_attention_pa_t_kernel(tc, x, pos0, pos1, wq, wk, out_0, out_1):
                 transpose_and_group(step)
             if 1 <= step <= STEPS:
                 sines(step - 1)
+            if 1 <= step and step + 1 < STEPS - 2 and step % 2 == 1:
+                sort_words(step + 1)
+            if 1 <= step <= STEPS:
                 project(step - 1)
+            if step == 2:
+                angles(slice(LATE_ANGLES, TILES))
             if step >= 2:
                 rotate_and_store(step - 2)
             if step < STEPS:
                 quantise(step)
             if step == 0:
-                angles(slice(FIRST_ANGLES, TILES))
+                angles(slice(FIRST_ANGLES, LATE_ANGLES))

import math
from contextlib import ExitStack

import concourse.mybir as mybir
from concourse.masks import make_identity

F32 = mybir.dt.float32
BF16 = mybir.dt.bfloat16
U32 = mybir.dt.uint32
U8 = mybir.dt.uint8
FP8X4 = mybir.dt.float8_e4m3fn_x4
ALU = mybir.AluOpType
ACT = mybir.ActivationFunctionType

P = 128
BATCH, ROWS, COLS = 32, 15, 17
TOKENS = 256
DIM = 1024
HEADS, PAIRS = 2, 32
FEATURES = HEADS * PAIRS * 2
FREQS = PAIRS // 2
BASE = 10000.0

QUARTERS = P // BATCH
TILES = TOKENS // QUARTERS
PACK = 4
PASSES = DIM // (P * PACK)
WORD_TILES = DIM // (2 * P)
STEP_TILES = 4
SHORT_TILES = STEP_TILES // 2
STEP_SIZES = [STEP_TILES] * (TILES // STEP_TILES - 1) + [SHORT_TILES] * 2
STEPS = len(STEP_SIZES)
STEP_STARTS = [sum(STEP_SIZES[:step]) for step in range(STEPS)]
BANK_TILES = 2
STEP_BANKS = STEP_TILES // BANK_TILES
WARM_COLUMNS = 512
LATE_ANGLES = 12 * STEP_TILES
LOADS_AHEAD = 7
FIRST_ANGLES = 4 * STEP_TILES

FLOPS = 2 * BATCH * TOKENS * DIM * 2 * FEATURES


def split_words(rows):
    return rows.bitcast(F32).rearrange("p (g w u) -> p g u w", g=PASSES, u=2)


def transpose_rows(nc, psum, words, identity):
    flipped = psum.tile([P, WORD_TILES, P], F32)
    for g in range(PASSES):
        for u in range(2):
            nc.tensor.transpose(flipped[:, 2 * g + u, :], words[:, g, u, :], identity)
    return flipped


def group_pairs(copy, grouped, flipped):
    copy(
        out=grouped.bitcast(F32),
        in_=flipped[:].rearrange("p (g u) r -> p g r u", u=2),
    )


def tile_attention_pa_t_kernel(tc, x, pos0, pos1, wq, wk, out_0, out_1):
    nc = tc.nc
    x_view = x.rearrange("b (r t) k -> (b r) t k", t=TILES)
    out_views = [o.rearrange("b (r t) h f -> (b r) t (h f)", t=TILES) for o in (out_0, out_1)]

    with ExitStack() as ctx:
        ctx.enter_context(tc.manual_schedule())
        const = ctx.enter_context(tc.tile_pool(name="const", bufs=1))
        x_pool = ctx.enter_context(tc.tile_pool(name="x_rows", bufs=LOADS_AHEAD + 1))
        work = ctx.enter_context(tc.tile_pool(name="work", bufs=3))
        out_pool = ctx.enter_context(tc.tile_pool(name="out_rows", bufs=5))
        flip_psum = ctx.enter_context(tc.psum_pool(name="flip_psum", bufs=4))

        pos0_rows = const.tile([BATCH, ROWS], BF16)
        pos1_rows = const.tile([BATCH, COLS], BF16)
        nc.sync.dma_start(out=pos0_rows[:], in_=pos0)
        nc.sync.dma_start(out=pos1_rows[:], in_=pos1)
        w_rows = const.tile([P, 2, DIM], BF16)
        nc.sync.dma_start(out=w_rows[:, 0, :], in_=wq)
        nc.sync.dma_start(out=w_rows[:, 1, :], in_=wk)

        def step_tiles(step):
            return slice(STEP_STARTS[step], STEP_STARTS[step] + STEP_SIZES[step])

        x_rows = {}

        def load(step):
            rows = x_pool.tile([P, STEP_SIZES[step], DIM], BF16, name="rows")
            run = 1 if step < 2 else STEP_SIZES[step]
            for first in range(0, STEP_SIZES[step], run):
                start = STEP_STARTS[step] + first
                nc.sync.dma_start(out=rows[:, first : first + run, :], in_=x_view[:, start : start + run, :])
            x_rows[step] = rows

        for step in range(LOADS_AHEAD):
            load(step)

        zeros = const.tile([P, WARM_COLUMNS], BF16)
        nc.vector.memset(zeros[:], 0.0)
        ones = const.tile([P, 1], F32)
        nc.vector.memset(ones[:], 1.0)
        quarter_turn = const.tile([P, 1], F32)
        nc.vector.tensor_scalar(out=quarter_turn[:], in0=ones[:], scalar1=math.pi / 2, scalar2=None, op0=ALU.mult)
        first_sin = const.tile([P, 1], F32)
        nc.scalar.activation(out=first_sin[:], in_=ones[:], func=ACT.Sin)
        identity = const.tile([P, P], F32)
        make_identity(nc, identity[:])
        send = const.tile([P, QUARTERS, BATCH, QUARTERS], BF16)
        nc.vector.memset(send[:], 0.0)
        for r in range(QUARTERS):
            nc.vector.tensor_copy(out=send[:, r, :, r], in_=identity[:, 0:BATCH])

        coords = const.tile([P, 2, TOKENS], BF16)
        nc.vector.memset(coords[:], 0.0)
        nc.vector.tensor_copy(
            out=coords[0:BATCH, 0, 1:TOKENS].rearrange("b (i j) -> b i j", j=COLS),
            in_=pos0_rows[:].unsqueeze(2).to_broadcast([BATCH, ROWS, COLS]),
        )
        nc.vector.tensor_copy(
            out=coords[0:BATCH, 1, 1:TOKENS].rearrange("b (i j) -> b i j", j=COLS),
            in_=pos1_rows[:].unsqueeze(1).to_broadcast([BATCH, ROWS, COLS]),
        )
        theta = const.tile([P, FREQS], F32)
        for m in range(FREQS):
            nc.vector.tensor_scalar(
                out=theta[:, m : m + 1], in0=ones[:], scalar1=1.0 / BASE ** (m / FREQS), scalar2=None, op0=ALU.mult
            )
        own_coords = const.tile([P, 2, TILES], F32)
        with tc.psum_pool(name="coord_psum", bufs=1) as coord_psum:
            idle_product = coord_psum.tile([P, WARM_COLUMNS], F32)

            def keep_clock_up(count):
                for turn in range(count):
                    nc.tensor.matmul(
                        out=idle_product[:], lhsT=zeros[:, 0:P], rhs=zeros[:], start=True, stop=True
                    )

            keep_clock_up(4)
            sent = coord_psum.tile([P, 2, TILES], F32)
            for axis in range(2):
                for r in range(QUARTERS):
                    nc.tensor.matmul(
                        out=sent[:, axis, :],
                        lhsT=send[:, r, :, :].rearrange("k b q -> k (b q)"),
                        rhs=coords[:, axis, r * TILES : (r + 1) * TILES],
                        start=(r == 0),
                        stop=(r == QUARTERS - 1),
                    )
            keep_clock_up(3)
            nc.vector.tensor_copy(out=own_coords[:], in_=sent[:])
        prod_psum = ctx.enter_context(tc.psum_pool(name="prod_psum", bufs=2 * STEP_BANKS))

        angle = const.tile([P, TILES, 2, FREQS], F32)
        trig = const.tile([P, TILES, 3, PAIRS], F32)
        def angles(tiles):
            spread = [P, tiles.stop - tiles.start, 2, FREQS]
            nc.vector.tensor_tensor(
                out=angle[:, tiles],
                in0=own_coords[:, :, tiles].rearrange("p a t -> p t a").unsqueeze(3).to_broadcast(spread),
                in1=theta[:].unsqueeze(1).unsqueeze(2).to_broadcast(spread),
                op=ALU.mult,
            )

        def sines(step):
            tiles = step_tiles(step)
            angle_pairs = angle[:, tiles].rearrange("p t a m -> p t (a m)")
            magnitude = work.tile([P, STEP_SIZES[step], PAIRS], F32, name="magnitude")
            nc.scalar.activation(out=magnitude[:], in_=angle_pairs, func=ACT.Abs)
            nc.scalar.activation(out=trig[:, tiles, 2, :], in_=angle_pairs, func=ACT.Sin)
            nc.scalar.activation(out=trig[:, tiles, 0, :], in_=angle_pairs, func=ACT.Sin, scale=-1.0)
            nc.scalar.activation(
                out=trig[:, tiles, 1, :], in_=magnitude[:], func=ACT.Sin, scale=-1.0, bias=quarter_turn[:]
            )

        angles(slice(0, FIRST_ANGLES))

        w_grouped = const.tile([P, PASSES, 2, P, PACK], BF16, align_bytes=64)
        for which in range(2):
            flipped = transpose_rows(nc, flip_psum, split_words(w_rows[:, which, :]), identity[:])
            group_pairs(nc.vector.tensor_copy, w_grouped[:, :, which, :, :], flipped)
        w_codes = const.tile([P, PASSES, 2 * P], U32, align_bytes=64)
        w_scales = const.tile([P, PASSES, 2 * P], U8, align_bytes=64)
        nc.vector.quantize_mx(
            out=w_codes[:].rearrange("p g n -> p (g n)").bitcast(FP8X4),
            scales=w_scales[:].rearrange("p g n -> p (g n)"),
            in_=w_grouped[:].rearrange("p g w n j -> p (g w n j)"),
        )

        grouped_rows = {}
        quantised = {}
        products = {}

        sorted_words = {}

        def sort_words(step):
            words = work.tile([P, PASSES, 2, P], F32, name="words")
            nc.scalar.copy(out=words[:], in_=split_words(x_rows[step][:, STEP_SIZES[step] - 1, :]))
            sorted_words[step] = words

        def transpose_and_group(step):
            grouped = work.tile([P, STEP_SIZES[step], PASSES, P, PACK], BF16, align_bytes=64, name="grouped")
            for i in range(STEP_SIZES[step]):
                if step in sorted_words and i == STEP_SIZES[step] - 1:
                    words = sorted_words[step][:]
                else:
                    words = split_words(x_rows[step][:, i, :])
                flipped = transpose_rows(nc, flip_psum, words, identity[:])
                group_pairs(nc.scalar.copy, grouped[:, i], flipped)
            grouped_rows[step] = grouped

        def quantise(step):
            codes = work.tile([P, STEP_SIZES[step], PASSES, P], U32, align_bytes=64, name="codes")
            scales = work.tile([P, STEP_SIZES[step], PASSES, P], U8, align_bytes=64, name="scales")
            run = SHORT_TILES if step == 0 else STEP_SIZES[step]
            for first in range(0, STEP_SIZES[step], run):
                tiles = slice(first, first + run)
                nc.vector.quantize_mx(
                    out=codes[:, tiles].rearrange("p t g r -> p (t g r)").bitcast(FP8X4),
                    scales=scales[:, tiles].rearrange("p t g r -> p (t g r)"),
                    in_=grouped_rows[step][:, tiles].rearrange("p t g r j -> p (t g r j)"),
                )
            quantised[step] = (codes, scales)

        def project(step):
            codes, scales = quantised[step]
            products[step] = []
            for bank in range(STEP_SIZES[step] // BANK_TILES):
                product = prod_psum.tile([P, BANK_TILES, 2 * HEADS, PAIRS, 2], F32, name="product")
                for j in range(BANK_TILES):
                    i = bank * BANK_TILES + j
                    for g in range(PASSES):
                        nc.tensor.matmul_mx(
                            out=product[:, j].rearrange("p c r e -> p (c r e)"),
                            lhsT=codes[:, i, g, :].bitcast(FP8X4),
                            lhsT_scale=scales[:, i, g, :],
                            rhs=w_codes[:, g, :].bitcast(FP8X4),
                            rhs_scale=w_scales[:, g, :],
                            start=(g == 0),
                            stop=(g == PASSES - 1),
                        )
                products[step].append(product)

        def multiply(step, i, results):
            product = products[step][i // BANK_TILES][:, i % BANK_TILES]
            spread = [P, 2 * HEADS, PAIRS, 2]
            for part, result, low_row in ((0, results[0], 1), (1, results[1], 0)):
                nc.vector.tensor_tensor(
                    out=result[:, i],
                    in0=product[:, :, :, part : part + 1].to_broadcast(spread),
                    in1=trig[:, STEP_STARTS[step] + i, low_row : low_row + 2, :]
                    .rearrange("p e r -> p r e")
                    .unsqueeze(1)
                    .to_broadcast(spread),
                    op=ALU.mult,
                )

        def add_and_store(engine, step, results, rotated):
            engine.tensor_tensor(
                out=rotated[:].rearrange("p w t f -> p t w f"),
                in0=results[0][:].rearrange("p t (w h) r e -> p t w (h r e)", w=2),
                in1=results[1][:].rearrange("p t (w h) r e -> p t w (h r e)", w=2),
                op=ALU.add,
            )
            for which in range(2):
                nc.sync.dma_start(out=out_views[which][:, step_tiles(step), :], in_=rotated[:, which])

        pending = []

        def rotate_and_store(step):
            size = STEP_SIZES[step]
            results = [
                work.tile([P, size, 2 * HEADS, PAIRS, 2], F32, name="from_re"),
                work.tile([P, size, 2 * HEADS, PAIRS, 2], F32, name="from_im"),
            ]
            rotated = out_pool.tile([P, 2, size, FEATURES], F32, name="rotated")
            for i in range(size):
                multiply(step, i, results)
            if size == STEP_TILES:
                add_and_store(nc.gpsimd, step, results, rotated)
            else:
                pending.append((step, results, rotated))
            if step == STEPS - 1:
                for late in pending:
                    add_and_store(nc.vector, *late)

        for step in range(STEPS + 2):
            if step + LOADS_AHEAD < STEPS:
                load(step + LOADS_AHEAD)
            if step < STEPS:
                transpose_and_group(step)
            if 1 <= step <= STEPS:
                sines(step - 1)
            if 1 <= step and step + 1 < STEPS - 2 and step % 2 == 1:
                sort_words(step + 1)
            if 1 <= step <= STEPS:
                project(step - 1)
            if step == 2:
                angles(slice(LATE_ANGLES, TILES))
            if step >= 2:
                rotate_and_store(step - 2)
            if step < STEPS:
                quantise(step)
            if step == 0:
                angles(slice(FIRST_ANGLES, LATE_ANGLES))
